import numpy as np
import ml_dtypes


def mxq(x, axis, fmt="e4m3"):
    dtype, down = {"e4m3": (ml_dtypes.float8_e4m3fn, 7), "e5m2": (ml_dtypes.float8_e5m2, 14)}[fmt]
    v = np.moveaxis(np.asarray(x, np.float32).astype(ml_dtypes.bfloat16).astype(np.float64), axis, -1)
    blocks = v.reshape(v.shape[:-1] + (-1, 32))
    amax = np.abs(blocks).max(-1, keepdims=True)
    byte = np.maximum(np.where(amax > 0, np.frexp(amax)[1] - 1 + 127, 0) - down, 1)
    scale = np.exp2(byte - 127.0)
    codes = (blocks / scale).astype(np.float32).astype(dtype).astype(np.float64)
    return np.moveaxis((codes * scale).reshape(v.shape), -1, axis)


WIDE = False


def mx_kscale(k):
    if not WIDE:
        return np.ones(k)
    levels = np.array([10, -10, 5, -5, 0])
    a = np.random.permutation(np.resize(levels, k // 512 * 4)).reshape(k // 512, 4)
    idx = np.arange(k)
    return np.exp2(a[idx // 512, idx % 128 // 32])


BF16 = ml_dtypes.bfloat16


def bf(x):
    return np.asarray(x, np.float32).astype(BF16)


def f64(x):
    return np.asarray(x).astype(np.float64)


E2M1 = np.array([0.0, 0.5, 1.0, 1.5, 2.0, 3.0, 4.0, 6.0, -0.0, -0.5, -1.0, -1.5, -2.0, -3.0, -4.0, -6.0])


def pack_weight(w, fmt):
    k, n = w.shape
    w = f64(bf(w)).reshape(k // 32, 32, n)
    amax = np.abs(w).max(1)
    if fmt == "e4m3":
        byte = np.frexp(amax)[1] - 1 + 127 - 7
    else:
        mant, ex = np.frexp(amax / 6.0)
        byte = np.where(mant > 0.5, ex, ex - 1) + 127
    byte = np.clip(np.where(amax > 0, byte, 1), 1, 254)
    scaled = (w * np.exp2(127.0 - byte)[:, None, :]).reshape(k, n).astype(np.float32)
    by_word = np.ascontiguousarray(scaled.reshape(k // 512, 128, 4, n).transpose(0, 1, 3, 2))
    if fmt == "e4m3":
        words = by_word.astype(ml_dtypes.float8_e4m3fn).view(np.uint8)
    else:
        c = by_word.astype(ml_dtypes.float4_e2m1fn).view(np.uint8) & 0xF
        words = c[..., 0::2] | (c[..., 1::2] << 4)
    return np.ascontiguousarray(words), np.ascontiguousarray(byte.astype(np.uint8).reshape(k // 512, 16, n))


def unpack_weight(words, scales, fmt):
    g, p, n, _ = words.shape
    if fmt == "e4m3":
        vals = np.ascontiguousarray(words).view(ml_dtypes.float8_e4m3fn).astype(np.float64)
    else:
        nib = np.empty((g, p, n, 4), np.uint8)
        nib[..., 0::2] = words & 0xF
        nib[..., 1::2] = words >> 4
        vals = E2M1[nib]
    vals = vals * np.repeat(np.exp2(scales.astype(np.float64) - 127.0), 8, axis=1)[..., None]
    return vals.transpose(0, 1, 3, 2).reshape(g * 512, n)

def pack4(w):
    words, scales = pack_weight(w, "e2m1")
    return words.reshape(words.shape[0], 128, -1), scales


def unpack4(words, scales):
    return unpack_weight(words.reshape(words.shape[0], 128, -1, 2), scales, "e2m1")


T, D, E = 1024, 6144, 768


def setup_inputs():
    s = mx_kscale(D)
    hidden_states = bf(np.random.standard_normal((T, D)) * s)
    weight = np.random.standard_normal((E, D)) * 1.0 / np.sqrt(D) / s[None, :]
    words, scales = pack4(np.ascontiguousarray(weight.T))
    return {"hidden_states": hidden_states,
            "weight_words": words,
            "weight_scales": scales}


def reference(hidden_states, weight_words, weight_scales):
    logits = mxq(f64(hidden_states), 1, "e4m3") @ unpack4(weight_words, weight_scales)
    return logits

@@ -1,0 +1,215 @@
+from contextlib import ExitStack
+
+import concourse.mybir as mybir
+from concourse.masks import make_identity
+
+BF16 = mybir.dt.bfloat16
+F32 = mybir.dt.float32
+I32 = mybir.dt.int32
+U8 = mybir.dt.uint8
+U32 = mybir.dt.uint32
+FP8X4 = mybir.dt.float8_e4m3fn_x4
+FP4X4 = mybir.dt.float4_e2m1fn_x4
+
+P = 128
+TOKENS, D, E = 1024, 6144, 768
+K_PASS = 512
+PASSES = D // K_PASS
+TILES = TOKENS // P
+CHUNKS = 3
+CHUNK_PASSES = PASSES // CHUNKS
+CHUNK_K = CHUNK_PASSES * K_PASS
+LOADS = 6
+
+FLOPS = 2 * TOKENS * D * E
+
+WORD_GROUPS = ((0, 1), (1, 2), (2, 4), (4, 6), (6, 8), (8, 10), (10, 12))
+
+
+def tile_longcatrouter_kernel(tc, hidden_states, weight_words, weight_scales, out):
+    nc = tc.nc
+    with ExitStack() as ctx:
+        const = ctx.enter_context(tc.tile_pool(name="const", bufs=1))
+        raw_pool = ctx.enter_context(tc.tile_pool(name="raw", bufs=1))
+        work = ctx.enter_context(tc.tile_pool(name="work", bufs=2 * CHUNKS))
+        outs = ctx.enter_context(tc.tile_pool(name="outs", bufs=3))
+        psum = ctx.enter_context(tc.psum_pool(name="psum", bufs=1))
+        ctx.enter_context(tc.manual_schedule())
+
+        w_scales = const.tile([P, PASSES, E], U8, align_bytes=64, name="w_scales")
+        nc.vector.memset(w_scales[:].rearrange("p g n -> p (g n)").bitcast(I32), 0)
+        ident = const.tile([P, P], F32, name="ident")
+        make_identity(nc, ident[:])
+
+        x_raw = {}
+
+        def load_x(i):
+            for h in range(CHUNKS):
+                t = raw_pool.tile([P, CHUNK_K], BF16, name="x_raw_%d_%d" % (i, h))
+                nc.sync.dma_start(
+                    out=t[:],
+                    in_=hidden_states[P * i : P * (i + 1), CHUNK_K * h : CHUNK_K * (h + 1)],
+                )
+                x_raw[(i, h)] = t
+
+        load_x(0)
+        load_x(1)
+
+        scales_by_row = weight_scales.rearrange("g q n -> q g n")
+        for half in range(2):
+            g0 = 6 * half
+            for b in range(2):
+                for r in range(4):
+                    nc.sync.dma_start(
+                        out=w_scales[32 * b + r : P : 64, g0 : g0 + 6, :].bitcast(I32),
+                        in_=scales_by_row[4 * b + r : 16 : 8, g0 : g0 + 6, :].bitcast(I32),
+                    )
+
+        words_by_part = weight_words.rearrange("g p b -> p g b")
+        w_words = {}
+        for g0, g1 in WORD_GROUPS:
+            t = const.tile([P, g1 - g0, 2 * E], U8, align_bytes=64, name="w_words_%d" % g0)
+            nc.sync.dma_start(out=t[:].bitcast(I32), in_=words_by_part[:, g0:g1, :].bitcast(I32))
+            for g in range(g0, g1):
+                w_words[g] = (t, g - g0)
+
+        for i in range(2, TILES):
+            load_x(i)
+
+        x_srt = {}
+        grouped = {}
+        codes = {}
+        x_scales = {}
+
+        def sort_words(i):
+            for h in range(CHUNKS):
+                t = work.tile([P, CHUNK_PASSES, 2, P], F32, tag="x_srt", name="x_srt")
+                nc.vector.tensor_copy(
+                    out=t[:],
+                    in_=x_raw[(i, h)][:].bitcast(F32).rearrange("t (g q u) -> t g u q", g=CHUNK_PASSES, q=P, u=2),
+                )
+                x_srt[(i, h)] = t
+
+        def transposes(i, b, is_sorted):
+            pt = psum.tile([P, 4, P], F32, tag="bank%d" % (2 + b), name="pt")
+            for j in range(4):
+                g = 2 * b + j // 2
+                u = j % 2
+                h, gl = g // CHUNK_PASSES, g % CHUNK_PASSES
+                if is_sorted:
+                    src = x_srt[(i, h)][:, gl, u, :]
+                else:
+                    src = x_raw[(i, h)][:, K_PASS * gl : K_PASS * (gl + 1)].bitcast(F32)[:, u : K_PASS // 2 : 2]
+                nc.tensor.transpose(pt[:, j, :], src, ident[:])
+            return pt
+
+        def copy_out(eng, i, b, pt):
+            h, half = b // 2, b % 2
+            dst = (
+                grouped[(i, h)][:, 1024 * half : 1024 * (half + 1)]
+                .bitcast(F32)
+                .rearrange("p (g t u) -> p g t u", g=2, t=P, u=2)
+            )
+            src = pt[:].rearrange("p (g u) t -> p g t u", u=2)
+            if eng == "S":
+                nc.scalar.copy(out=dst, in_=src)
+            else:
+                nc.vector.tensor_copy(out=dst, in_=src)
+
+        def quantise(i, h):
+            c = work.tile([P, CHUNK_PASSES * P], U32, tag="codes", name="codes", align_bytes=64)
+            s = work.tile([P, CHUNK_PASSES * P], U8, tag="x_scales", name="x_scales", align_bytes=64)
+            nc.vector.quantize_mx(out=c[:].bitcast(FP8X4), scales=s[:], in_=grouped[(i, h)][:])
+            codes[(i, h)] = c
+            x_scales[(i, h)] = s
+
+        def transpose_block(i, is_sorted, engines):
+            for b in range(LOADS):
+                if b % 2 == 0:
+                    grouped[(i, b // 2)] = work.tile(
+                        [P, CHUNK_K], BF16, tag="grouped", name="grouped", align_bytes=64
+                    )
+                pt = transposes(i, b, is_sorted)
+                copy_out(engines[b], i, b, pt)
+                if b == 3:
+                    quantise(i, 0)
+            quantise(i, 1)
+            quantise(i, 2)
+
+        def mx(acc, i, g, n0, n):
+            h, gl = g // CHUNK_PASSES, g % CHUNK_PASSES
+            wt, wg = w_words[g]
+            nc.tensor.matmul_mx(
+                out=acc,
+                lhsT=codes[(i, h)][:, P * gl : P * (gl + 1)].bitcast(FP8X4),
+                lhsT_scale=x_scales[(i, h)][:, P * gl : P * (gl + 1)],
+                rhs=wt[:, wg, 2 * n0 : 2 * (n0 + n)].bitcast(FP4X4),
+                rhs_scale=w_scales[:, g, n0 : n0 + n],
+                start=(g == 0),
+                stop=(g == PASSES - 1),
+            )
+
+        def group(acc, i, n0, n):
+            for g in range(PASSES):
+                mx(acc, i, g, n0, n)
+
+        out_sb = {}
+
+        def new_out(i):
+            out_sb[i] = outs.tile([P, E], F32, tag="out_sb", name="out_sb")
+
+        def store(i, c0, c1):
+            nc.sync.dma_start(out=out[P * i : P * (i + 1), c0:c1], in_=out_sb[i][:, c0:c1])
+
+        transpose_block(0, False, "SVSVSV")
+        transpose_block(1, False, "SVSVSV")
+        sort_words(2)
+
+        acc_a0 = psum.tile([P, 512], F32, tag="bank0", name="acc_a0")
+        acc_a1 = psum.tile([P, 512], F32, tag="bank2", name="acc_a1")
+        for g in range(PASSES):
+            mx(acc_a0[:], 0, g, 0, 512)
+            mx(acc_a1[:], 1, g, 0, 512)
+        new_out(0)
+        new_out(1)
+        nc.scalar.copy(out=out_sb[0][:, 0:512], in_=acc_a0[:])
+        nc.scalar.copy(out=out_sb[1][:, 0:512], in_=acc_a1[:])
+
+        acc_bc0 = psum.tile([P, 256], F32, tag="bank1", name="acc_bc0")
+        group(acc_bc0[:, 0:128], 0, 512, 128)
+        group(acc_bc0[:, 128:256], 0, 640, 128)
+        nc.scalar.copy(out=out_sb[0][:, 512:768], in_=acc_bc0[:])
+        store(0, 0, E)
+
+        acc_bc1 = psum.tile([P, 256], F32, tag="bank0", name="acc_bc1")
+        group(acc_bc1[:, 0:128], 1, 512, 128)
+        transpose_block(2, True, "SVSVSS")
+        group(acc_bc1[:, 128:256], 1, 640, 128)
+        nc.scalar.copy(out=out_sb[1][:, 512:768], in_=acc_bc1[:])
+        store(1, 0, E)
+
+        for i in range(2, TILES):
+            last = i == TILES - 1
+            if not last:
+                sort_words(i + 1)
+            acc_a = psum.tile([P, 512], F32, tag="bank1", name="acc_a")
+            group(acc_a[:], i, 0, 512)
+            new_out(i)
+            nc.scalar.copy(out=out_sb[i][:, 0:512], in_=acc_a[:])
+            if last:
+                store(i, 0, 512)
+            else:
+                transpose_block(i + 1, True, "SVSVSS")
+            acc_bc = psum.tile([P, 256], F32, tag="bank0", name="acc_bc")
+            group(acc_bc[:, 0:128], i, 512, 128)
+            if last:
+                nc.scalar.copy(out=out_sb[i][:, 512:640], in_=acc_bc[:, 0:128])
+                store(i, 512, 640)
+                acc_c = psum.tile([P, 128], F32, tag="bank2", name="acc_c")
+                group(acc_c[:], i, 640, 128)
+                nc.vector.tensor_copy(out=out_sb[i][:, 640:768], in_=acc_c[:])
+                store(i, 640, 768)
+            else:
+                group(acc_bc[:, 128:256], i, 640, 128)
+                nc.scalar.copy(out=out_sb[i][:, 512:768], in_=acc_bc[:])
+                store(i, 0, E)

@@ -10,20 +10,25 @@ U8 = mybir.dt.uint8
 U32 = mybir.dt.uint32
 FP8X4 = mybir.dt.float8_e4m3fn_x4
 FP4X4 = mybir.dt.float4_e2m1fn_x4
+ADD = mybir.AluOpType.add
 
 P = 128
 TOKENS, D, E = 1024, 6144, 768
 K_PASS = 512
-PASSES = D // K_PASS
 TILES = TOKENS // P
-CHUNKS = 3
-CHUNK_PASSES = PASSES // CHUNKS
-CHUNK_K = CHUNK_PASSES * K_PASS
-LOADS = 6
+ROUNDS = 2
+UNIT_PASSES = 6
+UNIT_K = UNIT_PASSES * K_PASS
+UNIT_LOADS = UNIT_PASSES // 2
+LOAD_K = 2 * K_PASS
+UNITS = ROUNDS * TILES
+PARTS = ((0, 4), (4, 2))
 
 FLOPS = 2 * TOKENS * D * E
 
-WORD_GROUPS = ((0, 1), (1, 2), (2, 4), (4, 6), (6, 8), (8, 10), (10, 12))
+WORD_GROUPS = ((0, 1), (1, 3), (3, 6), (6, 9), (9, 12))
+RAW_SPLITS = {0: (4, 2), 1: (4, 2), 2: (4, 2)}
+BUNCHES = ((0, 1), (2,), (3, 4), (5, 6), (7, 8), (9, 10), (11, 12), (13, 14), (15,))
 
 
 def tile_longcatrouter_kernel(tc, hidden_states, weight_words, weight_scales, out):
@@ -31,185 +36,212 @@ def tile_longcatrouter_kernel(tc, hidden_states, weight_words, weight_scales, ou
     with ExitStack() as ctx:
         const = ctx.enter_context(tc.tile_pool(name="const", bufs=1))
         raw_pool = ctx.enter_context(tc.tile_pool(name="raw", bufs=1))
-        work = ctx.enter_context(tc.tile_pool(name="work", bufs=2 * CHUNKS))
-        outs = ctx.enter_context(tc.tile_pool(name="outs", bufs=3))
+        srt_pool = ctx.enter_context(tc.tile_pool(name="srt", bufs=9))
+        grp_pool = ctx.enter_context(tc.tile_pool(name="grp", bufs=3))
+        code_pool = ctx.enter_context(tc.tile_pool(name="code", bufs=4))
         psum = ctx.enter_context(tc.psum_pool(name="psum", bufs=1))
         ctx.enter_context(tc.manual_schedule())
 
-        w_scales = const.tile([P, PASSES, E], U8, align_bytes=64, name="w_scales")
-        nc.vector.memset(w_scales[:].rearrange("p g n -> p (g n)").bitcast(I32), 0)
+        w_scales = []
+        for r in range(ROUNDS):
+            t = const.tile([P, UNIT_PASSES, E], U8, align_bytes=64, name="w_scales_%d" % r)
+            nc.vector.memset(t[:].rearrange("p g n -> p (g n)").bitcast(I32), 0)
+            w_scales.append(t)
         ident = const.tile([P, P], F32, name="ident")
         make_identity(nc, ident[:])
 
         x_raw = {}
 
-        def load_x(i):
-            for h in range(CHUNKS):
-                t = raw_pool.tile([P, CHUNK_K], BF16, name="x_raw_%d_%d" % (i, h))
-                nc.sync.dma_start(
-                    out=t[:],
-                    in_=hidden_states[P * i : P * (i + 1), CHUNK_K * h : CHUNK_K * (h + 1)],
-                )
-                x_raw[(i, h)] = t
-
-        load_x(0)
-        load_x(1)
+        def load_x(u):
+            r, i = u // TILES, u % TILES
+            first = 0
+            for passes in RAW_SPLITS.get(u, (UNIT_PASSES,)):
+                t = raw_pool.tile([P, passes * K_PASS], BF16, name="x_raw_%d_%d" % (u, first))
+                k0 = r * UNIT_K + first * K_PASS
+                nc.sync.dma_start(out=t[:], in_=hidden_states[P * i : P * (i + 1), k0 : k0 + passes * K_PASS])
+                for j in range(passes // 2):
+                    x_raw[(u, first // 2 + j)] = t[:, LOAD_K * j : LOAD_K * (j + 1)]
+                first += passes
 
         scales_by_row = weight_scales.rearrange("g q n -> q g n")
-        for half in range(2):
-            g0 = 6 * half
-            for b in range(2):
-                for r in range(4):
-                    nc.sync.dma_start(
-                        out=w_scales[32 * b + r : P : 64, g0 : g0 + 6, :].bitcast(I32),
-                        in_=scales_by_row[4 * b + r : 16 : 8, g0 : g0 + 6, :].bitcast(I32),
-                    )
+
+        def load_scales(r):
+            g0 = r * UNIT_PASSES
+            for row in range(4):
+                nc.sync.dma_start(
+                    out=w_scales[r][row:P:32, :, :].bitcast(I32),
+                    in_=scales_by_row[row:16:4, g0 : g0 + UNIT_PASSES, :].bitcast(I32),
+                )
 
         words_by_part = weight_words.rearrange("g p b -> p g b")
         w_words = {}
-        for g0, g1 in WORD_GROUPS:
+
+        def load_words(g0, g1):
             t = const.tile([P, g1 - g0, 2 * E], U8, align_bytes=64, name="w_words_%d" % g0)
             nc.sync.dma_start(out=t[:].bitcast(I32), in_=words_by_part[:, g0:g1, :].bitcast(I32))
             for g in range(g0, g1):
                 w_words[g] = (t, g - g0)
 
-        for i in range(2, TILES):
-            load_x(i)
+        load_x(0)
+        load_scales(0)
+        load_x(1)
+        for g0, g1 in WORD_GROUPS[:3]:
+            load_words(g0, g1)
+        for u in range(2, TILES):
+            load_x(u)
+        load_scales(1)
+        for g0, g1 in WORD_GROUPS[3:]:
+            load_words(g0, g1)
+        for u in range(TILES, UNITS):
+            load_x(u)
+
+        sums = [const.tile([P, E], F32, name="sums_%d" % i) for i in range(TILES)]
 
         x_srt = {}
         grouped = {}
         codes = {}
         x_scales = {}
 
-        def sort_words(i):
-            for h in range(CHUNKS):
-                t = work.tile([P, CHUNK_PASSES, 2, P], F32, tag="x_srt", name="x_srt")
+        def sort_words(u):
+            for l in range(UNIT_LOADS):
+                t = srt_pool.tile([P, 2, 2, P], F32, tag="x_srt", name="x_srt")
                 nc.vector.tensor_copy(
                     out=t[:],
-                    in_=x_raw[(i, h)][:].bitcast(F32).rearrange("t (g q u) -> t g u q", g=CHUNK_PASSES, q=P, u=2),
+                    in_=x_raw[(u, l)].bitcast(F32).rearrange("t (g q u) -> t g u q", g=2, q=P, u=2),
                 )
-                x_srt[(i, h)] = t
+                x_srt[(u, l)] = t
 
-        def transposes(i, b, is_sorted):
-            pt = psum.tile([P, 4, P], F32, tag="bank%d" % (2 + b), name="pt")
+        def transpose_load(u, l, bank):
+            pt = psum.tile([P, 4, P], F32, tag="bank%d" % bank, name="pt")
             for j in range(4):
-                g = 2 * b + j // 2
-                u = j % 2
-                h, gl = g // CHUNK_PASSES, g % CHUNK_PASSES
-                if is_sorted:
-                    src = x_srt[(i, h)][:, gl, u, :]
-                else:
-                    src = x_raw[(i, h)][:, K_PASS * gl : K_PASS * (gl + 1)].bitcast(F32)[:, u : K_PASS // 2 : 2]
-                nc.tensor.transpose(pt[:, j, :], src, ident[:])
-            return pt
-
-        def copy_out(eng, i, b, pt):
-            h, half = b // 2, b % 2
-            dst = (
-                grouped[(i, h)][:, 1024 * half : 1024 * (half + 1)]
-                .bitcast(F32)
-                .rearrange("p (g t u) -> p g t u", g=2, t=P, u=2)
+                nc.tensor.transpose(pt[:, j, :], x_srt[(u, l)][:, j // 2, j % 2, :], ident[:])
+            part = 0 if l < 2 else 1
+            if l in (0, 2):
+                grouped[(u, part)] = grp_pool.tile(
+                    [P, PARTS[part][1] * K_PASS], BF16, tag="grouped%d" % part, name="grouped", align_bytes=64
+                )
+            at = LOAD_K * (l % 2)
+            nc.scalar.copy(
+                out=grouped[(u, part)][:, at : at + LOAD_K].bitcast(F32).rearrange("p (g t u) -> p g t u", g=2, t=P, u=2),
+                in_=pt[:].rearrange("p (g u) t -> p g t u", u=2),
             )
-            src = pt[:].rearrange("p (g u) t -> p g t u", u=2)
-            if eng == "S":
-                nc.scalar.copy(out=dst, in_=src)
-            else:
-                nc.vector.tensor_copy(out=dst, in_=src)
 
-        def quantise(i, h):
-            c = work.tile([P, CHUNK_PASSES * P], U32, tag="codes", name="codes", align_bytes=64)
-            s = work.tile([P, CHUNK_PASSES * P], U8, tag="x_scales", name="x_scales", align_bytes=64)
-            nc.vector.quantize_mx(out=c[:].bitcast(FP8X4), scales=s[:], in_=grouped[(i, h)][:])
-            codes[(i, h)] = c
-            x_scales[(i, h)] = s
+        def transpose_bunch(units):
+            banks = (2, 3, 4, 5, 6, 7) if len(units) == 2 else (3, 4, 5)
+            at = 0
+            for u in units:
+                for l in range(UNIT_LOADS):
+                    transpose_load(u, l, banks[at])
+                    at += 1
 
-        def transpose_block(i, is_sorted, engines):
-            for b in range(LOADS):
-                if b % 2 == 0:
-                    grouped[(i, b // 2)] = work.tile(
-                        [P, CHUNK_K], BF16, tag="grouped", name="grouped", align_bytes=64
-                    )
-                pt = transposes(i, b, is_sorted)
-                copy_out(engines[b], i, b, pt)
-                if b == 3:
-                    quantise(i, 0)
-            quantise(i, 1)
-            quantise(i, 2)
+        def quantise(u):
+            for part in range(len(PARTS)):
+                width = PARTS[part][1] * P
+                c = code_pool.tile([P, width], U32, tag="codes%d" % part, name="codes", align_bytes=64)
+                s = code_pool.tile([P, width], U8, tag="x_scales%d" % part, name="x_scales", align_bytes=64)
+                nc.vector.quantize_mx(out=c[:].bitcast(FP8X4), scales=s[:], in_=grouped[(u, part)][:])
+                codes[(u, part)] = c
+                x_scales[(u, part)] = s
 
-        def mx(acc, i, g, n0, n):
-            h, gl = g // CHUNK_PASSES, g % CHUNK_PASSES
-            wt, wg = w_words[g]
+        def mx(acc, u, gl, n0, n):
+            r = u // TILES
+            part = 0 if gl < 4 else 1
+            at = P * (gl - PARTS[part][0])
+            wt, wg = w_words[r * UNIT_PASSES + gl]
             nc.tensor.matmul_mx(
                 out=acc,
-                lhsT=codes[(i, h)][:, P * gl : P * (gl + 1)].bitcast(FP8X4),
-                lhsT_scale=x_scales[(i, h)][:, P * gl : P * (gl + 1)],
+                lhsT=codes[(u, part)][:, at : at + P].bitcast(FP8X4),
+                lhsT_scale=x_scales[(u, part)][:, at : at + P],
                 rhs=wt[:, wg, 2 * n0 : 2 * (n0 + n)].bitcast(FP4X4),
-                rhs_scale=w_scales[:, g, n0 : n0 + n],
-                start=(g == 0),
-                stop=(g == PASSES - 1),
+                rhs_scale=w_scales[r][:, gl, n0 : n0 + n],
+                start=(gl == 0),
+                stop=(gl == UNIT_PASSES - 1),
             )
 
-        def group(acc, i, n0, n):
-            for g in range(PASSES):
-                mx(acc, i, g, n0, n)
+        def group(acc, u, n0, n):
+            for gl in range(UNIT_PASSES):
+                mx(acc, u, gl, n0, n)
 
-        out_sb = {}
+        def evacuate(u, acc, c0, c1, on_scalar=False):
+            dst = sums[u % TILES][:, c0:c1]
+            if u >= TILES:
+                nc.vector.tensor_tensor(out=dst, in0=acc, in1=dst, op=ADD)
+            elif on_scalar:
+                nc.scalar.copy(out=dst, in_=acc)
+            else:
+                nc.vector.tensor_copy(out=dst, in_=acc)
 
-        def new_out(i):
-            out_sb[i] = outs.tile([P, E], F32, tag="out_sb", name="out_sb")
+        def store(u, c0, c1):
+            i = u % TILES
+            nc.sync.dma_start(out=out[P * i : P * (i + 1), c0:c1], in_=sums[i][:, c0:c1])
 
-        def store(i, c0, c1):
-            nc.sync.dma_start(out=out[P * i : P * (i + 1), c0:c1], in_=out_sb[i][:, c0:c1])
+        def bank_a(u):
+            return psum.tile([P, 512], F32, tag="bank%d" % (1 + u % 2), name="acc_a")
 
-        transpose_block(0, False, "SVSVSV")
-        transpose_block(1, False, "SVSVSV")
+        for u in BUNCHES[0]:
+            sort_words(u)
+            for l in range(UNIT_LOADS):
+                transpose_load(u, l, 2 + UNIT_LOADS * u + l)
+            quantise(u)
         sort_words(2)
 
-        acc_a0 = psum.tile([P, 512], F32, tag="bank0", name="acc_a0")
-        acc_a1 = psum.tile([P, 512], F32, tag="bank2", name="acc_a1")
-        for g in range(PASSES):
-            mx(acc_a0[:], 0, g, 0, 512)
-            mx(acc_a1[:], 1, g, 0, 512)
-        new_out(0)
-        new_out(1)
-        nc.scalar.copy(out=out_sb[0][:, 0:512], in_=acc_a0[:])
-        nc.scalar.copy(out=out_sb[1][:, 0:512], in_=acc_a1[:])
+        acc_a0 = bank_a(0)
+        acc_a1 = bank_a(1)
+        for first in (0, 3):
+            for u, acc in ((0, acc_a0), (1, acc_a1)):
+                for gl in range(first, first + 3):
+                    mx(acc[:], u, gl, 0, 512)
+        evacuate(0, acc_a0[:], 0, 512, on_scalar=True)
+        evacuate(1, acc_a1[:], 0, 512, on_scalar=True)
 
-        acc_bc0 = psum.tile([P, 256], F32, tag="bank1", name="acc_bc0")
+        acc_bc0 = psum.tile([P, 256], F32, tag="bank0", name="acc_bc")
         group(acc_bc0[:, 0:128], 0, 512, 128)
+        transpose_bunch(BUNCHES[1])
+        quantise(2)
         group(acc_bc0[:, 128:256], 0, 640, 128)
-        nc.scalar.copy(out=out_sb[0][:, 512:768], in_=acc_bc0[:])
-        store(0, 0, E)
-
-        acc_bc1 = psum.tile([P, 256], F32, tag="bank0", name="acc_bc1")
+        evacuate(0, acc_bc0[:], 512, 768)
+        acc_bc1 = psum.tile([P, 256], F32, tag="bank7", name="acc_bc")
         group(acc_bc1[:, 0:128], 1, 512, 128)
-        transpose_block(2, True, "SVSVSS")
         group(acc_bc1[:, 128:256], 1, 640, 128)
-        nc.scalar.copy(out=out_sb[1][:, 512:768], in_=acc_bc1[:])
-        store(1, 0, E)
+        sort_words(3)
+        evacuate(1, acc_bc1[:], 512, 768)
+        sort_words(4)
+        next_sort = 5
 
-        for i in range(2, TILES):
-            last = i == TILES - 1
-            if not last:
-                sort_words(i + 1)
-            acc_a = psum.tile([P, 512], F32, tag="bank1", name="acc_a")
-            group(acc_a[:], i, 0, 512)
-            new_out(i)
-            nc.scalar.copy(out=out_sb[i][:, 0:512], in_=acc_a[:])
-            if last:
-                store(i, 0, 512)
-            else:
-                transpose_block(i + 1, True, "SVSVSS")
-            acc_bc = psum.tile([P, 256], F32, tag="bank0", name="acc_bc")
-            group(acc_bc[:, 0:128], i, 512, 128)
-            if last:
-                nc.scalar.copy(out=out_sb[i][:, 512:640], in_=acc_bc[:, 0:128])
-                store(i, 512, 640)
-                acc_c = psum.tile([P, 128], F32, tag="bank2", name="acc_c")
-                group(acc_c[:], i, 640, 128)
-                nc.vector.tensor_copy(out=out_sb[i][:, 640:768], in_=acc_c[:])
-                store(i, 640, 768)
-            else:
-                group(acc_bc[:, 128:256], i, 640, 128)
-                nc.scalar.copy(out=out_sb[i][:, 512:768], in_=acc_bc[:])
-                store(i, 0, E)
+        for j in range(1, len(BUNCHES)):
+            units = BUNCHES[j]
+            following = BUNCHES[j + 1] if j + 1 < len(BUNCHES) else ()
+            for u in units:
+                closes_bunch = u == units[-1]
+                very_last = u == UNITS - 1
+                acc_a = bank_a(u)
+                group(acc_a[:], u, 0, 512)
+                evacuate(u, acc_a[:], 0, 512)
+                if very_last:
+                    store(u, 0, 512)
+                if closes_bunch and following:
+                    transpose_bunch(following)
+                    quantise(following[0])
+                if not closes_bunch and next_sort < UNITS:
+                    sort_words(next_sort)
+                    next_sort += 1
+                acc_bc = psum.tile([P, 256], F32, tag="bank0", name="acc_bc")
+                group(acc_bc[:, 0:128], u, 512, 128)
+                if very_last:
+                    evacuate(u, acc_bc[:, 0:128], 512, 640)
+                    store(u, 512, 640)
+                    acc_c = psum.tile([P, 128], F32, tag="bank7", name="acc_c")
+                    group(acc_c[:], u, 640, 128)
+                    evacuate(u, acc_c[:], 640, 768)
+                    store(u, 640, 768)
+                else:
+                    group(acc_bc[:, 128:256], u, 640, 128)
+                    evacuate(u, acc_bc[:], 512, 768)
+                    if u >= TILES:
+                        store(u, 0, E)
+                if closes_bunch:
+                    for v in following[1:]:
+                        quantise(v)
+                    if next_sort < UNITS:
+                        sort_words(next_sort)
+                        next_sort += 1

@@ -23,12 +23,11 @@ UNIT_LOADS = UNIT_PASSES // 2
 LOAD_K = 2 * K_PASS
 UNITS = ROUNDS * TILES
 PARTS = ((0, 4), (4, 2))
+BANKS = 8
 
 FLOPS = 2 * TOKENS * D * E
 
-WORD_GROUPS = ((0, 1), (1, 3), (3, 6), (6, 9), (9, 12))
 RAW_SPLITS = {0: (4, 2), 1: (4, 2), 2: (4, 2)}
-BUNCHES = ((0, 1), (2,), (3, 4), (5, 6), (7, 8), (9, 10), (11, 12), (13, 14), (15,))
 
 
 def tile_longcatrouter_kernel(tc, hidden_states, weight_words, weight_scales, out):
@@ -36,7 +35,7 @@ def tile_longcatrouter_kernel(tc, hidden_states, weight_words, weight_scales, ou
     with ExitStack() as ctx:
         const = ctx.enter_context(tc.tile_pool(name="const", bufs=1))
         raw_pool = ctx.enter_context(tc.tile_pool(name="raw", bufs=1))
-        srt_pool = ctx.enter_context(tc.tile_pool(name="srt", bufs=9))
+        srt_pool = ctx.enter_context(tc.tile_pool(name="srt", bufs=12))
         grp_pool = ctx.enter_context(tc.tile_pool(name="grp", bufs=3))
         code_pool = ctx.enter_context(tc.tile_pool(name="code", bufs=4))
         psum = ctx.enter_context(tc.psum_pool(name="psum", bufs=1))
@@ -83,15 +82,17 @@ def tile_longcatrouter_kernel(tc, hidden_states, weight_words, weight_scales, ou
                 w_words[g] = (t, g - g0)
 
         load_x(0)
-        load_scales(0)
         load_x(1)
-        for g0, g1 in WORD_GROUPS[:3]:
-            load_words(g0, g1)
-        for u in range(2, TILES):
+        load_scales(0)
+        load_words(0, 1)
+        load_words(1, 3)
+        load_x(2)
+        load_words(3, 6)
+        for u in range(3, TILES):
             load_x(u)
         load_scales(1)
-        for g0, g1 in WORD_GROUPS[3:]:
-            load_words(g0, g1)
+        load_words(6, 9)
+        load_words(9, 12)
         for u in range(TILES, UNITS):
             load_x(u)
 
@@ -101,18 +102,30 @@ def tile_longcatrouter_kernel(tc, hidden_states, weight_words, weight_scales, ou
         grouped = {}
         codes = {}
         x_scales = {}
+        state = {"free": list(range(BANKS)), "sorted": 0}
 
-        def sort_words(u):
-            for l in range(UNIT_LOADS):
+        def take_bank(shape, name):
+            bank = state["free"][0]
+            state["free"] = state["free"][1:]
+            return bank, psum.tile(shape, F32, tag="bank%d" % bank, name=name)
+
+        def give_bank(bank):
+            state["free"] = state["free"] + [bank]
+
+        def sort_loads(count):
+            for n in range(state["sorted"], min(state["sorted"] + count, UNITS * UNIT_LOADS)):
                 t = srt_pool.tile([P, 2, 2, P], F32, tag="x_srt", name="x_srt")
                 nc.vector.tensor_copy(
                     out=t[:],
-                    in_=x_raw[(u, l)].bitcast(F32).rearrange("t (g q u) -> t g u q", g=2, q=P, u=2),
+                    in_=x_raw[(n // UNIT_LOADS, n % UNIT_LOADS)]
+                    .bitcast(F32)
+                    .rearrange("t (g q u) -> t g u q", g=2, q=P, u=2),
                 )
-                x_srt[(u, l)] = t
+                x_srt[(n // UNIT_LOADS, n % UNIT_LOADS)] = t
+            state["sorted"] = state["sorted"] + count
 
-        def transpose_load(u, l, bank):
-            pt = psum.tile([P, 4, P], F32, tag="bank%d" % bank, name="pt")
+        def transpose_load(u, l, eng):
+            bank, pt = take_bank([P, 4, P], "pt")
             for j in range(4):
                 nc.tensor.transpose(pt[:, j, :], x_srt[(u, l)][:, j // 2, j % 2, :], ident[:])
             part = 0 if l < 2 else 1
@@ -121,27 +134,25 @@ def tile_longcatrouter_kernel(tc, hidden_states, weight_words, weight_scales, ou
                     [P, PARTS[part][1] * K_PASS], BF16, tag="grouped%d" % part, name="grouped", align_bytes=64
                 )
             at = LOAD_K * (l % 2)
-            nc.scalar.copy(
-                out=grouped[(u, part)][:, at : at + LOAD_K].bitcast(F32).rearrange("p (g t u) -> p g t u", g=2, t=P, u=2),
-                in_=pt[:].rearrange("p (g u) t -> p g t u", u=2),
-            )
+            dst = grouped[(u, part)][:, at : at + LOAD_K].bitcast(F32).rearrange("p (g t u) -> p g t u", g=2, t=P, u=2)
+            src = pt[:].rearrange("p (g u) t -> p g t u", u=2)
+            if eng == "S":
+                nc.scalar.copy(out=dst, in_=src)
+            else:
+                nc.vector.tensor_copy(out=dst, in_=src)
+            give_bank(bank)
 
-        def transpose_bunch(units):
-            banks = (2, 3, 4, 5, 6, 7) if len(units) == 2 else (3, 4, 5)
-            at = 0
-            for u in units:
-                for l in range(UNIT_LOADS):
-                    transpose_load(u, l, banks[at])
-                    at += 1
+        def transpose_unit(u, engines="SSS"):
+            for l in range(UNIT_LOADS):
+                transpose_load(u, l, engines[l])
 
-        def quantise(u):
-            for part in range(len(PARTS)):
-                width = PARTS[part][1] * P
-                c = code_pool.tile([P, width], U32, tag="codes%d" % part, name="codes", align_bytes=64)
-                s = code_pool.tile([P, width], U8, tag="x_scales%d" % part, name="x_scales", align_bytes=64)
-                nc.vector.quantize_mx(out=c[:].bitcast(FP8X4), scales=s[:], in_=grouped[(u, part)][:])
-                codes[(u, part)] = c
-                x_scales[(u, part)] = s
+        def quantise(u, part):
+            width = PARTS[part][1] * P
+            c = code_pool.tile([P, width], U32, tag="codes%d" % part, name="codes", align_bytes=64)
+            s = code_pool.tile([P, width], U8, tag="x_scales%d" % part, name="x_scales", align_bytes=64)
+            nc.vector.quantize_mx(out=c[:].bitcast(FP8X4), scales=s[:], in_=grouped[(u, part)][:])
+            codes[(u, part)] = c
+            x_scales[(u, part)] = s
 
         def mx(acc, u, gl, n0, n):
             r = u // TILES
@@ -162,11 +173,11 @@ def tile_longcatrouter_kernel(tc, hidden_states, weight_words, weight_scales, ou
             for gl in range(UNIT_PASSES):
                 mx(acc, u, gl, n0, n)
 
-        def evacuate(u, acc, c0, c1, on_scalar=False):
+        def evacuate(u, acc, c0, c1, eng="V"):
             dst = sums[u % TILES][:, c0:c1]
             if u >= TILES:
                 nc.vector.tensor_tensor(out=dst, in0=acc, in1=dst, op=ADD)
-            elif on_scalar:
+            elif eng == "S":
                 nc.scalar.copy(out=dst, in_=acc)
             else:
                 nc.vector.tensor_copy(out=dst, in_=acc)
@@ -175,73 +186,81 @@ def tile_longcatrouter_kernel(tc, hidden_states, weight_words, weight_scales, ou
             i = u % TILES
             nc.sync.dma_start(out=out[P * i : P * (i + 1), c0:c1], in_=sums[i][:, c0:c1])
 
-        def bank_a(u):
-            return psum.tile([P, 512], F32, tag="bank%d" % (1 + u % 2), name="acc_a")
+        def columns_a(u):
+            bank, acc = take_bank([P, 512], "acc_a")
+            group(acc[:], u, 0, 512)
+            evacuate(u, acc[:], 0, 512)
+            give_bank(bank)
 
-        for u in BUNCHES[0]:
-            sort_words(u)
-            for l in range(UNIT_LOADS):
-                transpose_load(u, l, 2 + UNIT_LOADS * u + l)
-            quantise(u)
-        sort_words(2)
+        def columns_bc(u):
+            bank, acc = take_bank([P, 256], "acc_bc")
+            group(acc[:, 0:128], u, 512, 128)
+            group(acc[:, 128:256], u, 640, 128)
+            evacuate(u, acc[:], 512, 768)
+            give_bank(bank)
+            if u >= TILES:
+                store(u, 0, E)
 
-        acc_a0 = bank_a(0)
-        acc_a1 = bank_a(1)
-        for first in (0, 3):
-            for u, acc in ((0, acc_a0), (1, acc_a1)):
-                for gl in range(first, first + 3):
-                    mx(acc[:], u, gl, 0, 512)
-        evacuate(0, acc_a0[:], 0, 512, on_scalar=True)
-        evacuate(1, acc_a1[:], 0, 512, on_scalar=True)
+        sort_loads(6)
+        transpose_unit(0)
+        quantise(0, 0)
+        quantise(0, 1)
+        transpose_unit(1)
+        quantise(1, 0)
+        quantise(1, 1)
+        sort_loads(3)
 
-        acc_bc0 = psum.tile([P, 256], F32, tag="bank0", name="acc_bc")
-        group(acc_bc0[:, 0:128], 0, 512, 128)
-        transpose_bunch(BUNCHES[1])
-        quantise(2)
-        group(acc_bc0[:, 128:256], 0, 640, 128)
-        evacuate(0, acc_bc0[:], 512, 768)
-        acc_bc1 = psum.tile([P, 256], F32, tag="bank7", name="acc_bc")
-        group(acc_bc1[:, 0:128], 1, 512, 128)
-        group(acc_bc1[:, 128:256], 1, 640, 128)
-        sort_words(3)
-        evacuate(1, acc_bc1[:], 512, 768)
-        sort_words(4)
-        next_sort = 5
+        head = []
+        for u, n0, n in ((0, 0, 512), (0, 512, 128), (0, 640, 128), (1, 0, 512), (1, 512, 128)):
+            bank, acc = take_bank([P, n], "acc_head")
+            head.append((u, n0, n, bank, acc))
+        for gl in range(3):
+            for u, n0, n, bank, acc in head:
+                mx(acc[:], u, gl, n0, n)
+        transpose_unit(2)
+        quantise(2, 0)
+        quantise(2, 1)
+        sort_loads(3)
+        for gl in range(3, UNIT_PASSES):
+            for u, n0, n, bank, acc in head:
+                mx(acc[:], u, gl, n0, n)
+        for at in (1, 4, 2):
+            u, n0, n, bank, acc = head[at]
+            evacuate(u, acc[:], n0, n0 + n, "V" if u == 0 else "S")
+            give_bank(bank)
+        bank_c1, acc_c1 = take_bank([P, 128], "acc_head")
+        group(acc_c1[:], 1, 640, 128)
+        for at in (0, 3):
+            u, n0, n, bank, acc = head[at]
+            evacuate(u, acc[:], n0, n0 + n, "V" if u == 0 else "S")
+            give_bank(bank)
+        evacuate(1, acc_c1[:], 640, 768, "S")
+        give_bank(bank_c1)
+        sort_loads(3)
 
-        for j in range(1, len(BUNCHES)):
-            units = BUNCHES[j]
-            following = BUNCHES[j + 1] if j + 1 < len(BUNCHES) else ()
-            for u in units:
-                closes_bunch = u == units[-1]
-                very_last = u == UNITS - 1
-                acc_a = bank_a(u)
-                group(acc_a[:], u, 0, 512)
-                evacuate(u, acc_a[:], 0, 512)
-                if very_last:
-                    store(u, 0, 512)
-                if closes_bunch and following:
-                    transpose_bunch(following)
-                    quantise(following[0])
-                if not closes_bunch and next_sort < UNITS:
-                    sort_words(next_sort)
-                    next_sort += 1
-                acc_bc = psum.tile([P, 256], F32, tag="bank0", name="acc_bc")
-                group(acc_bc[:, 0:128], u, 512, 128)
-                if very_last:
-                    evacuate(u, acc_bc[:, 0:128], 512, 640)
-                    store(u, 512, 640)
-                    acc_c = psum.tile([P, 128], F32, tag="bank7", name="acc_c")
-                    group(acc_c[:], u, 640, 128)
-                    evacuate(u, acc_c[:], 640, 768)
-                    store(u, 640, 768)
-                else:
-                    group(acc_bc[:, 128:256], u, 640, 128)
-                    evacuate(u, acc_bc[:], 512, 768)
-                    if u >= TILES:
-                        store(u, 0, E)
-                if closes_bunch:
-                    for v in following[1:]:
-                        quantise(v)
-                    if next_sort < UNITS:
-                        sort_words(next_sort)
-                        next_sort += 1
+        for first in range(2, UNITS, 2):
+            bunch = [u for u in (first + 1, first + 2) if u < UNITS]
+            for u in bunch:
+                transpose_unit(u)
+            quantise(bunch[0], 0)
+            quantise(bunch[0], 1)
+            sort_loads(2)
+            columns_a(first)
+            if len(bunch) > 1:
+                quantise(bunch[1], 0)
+                quantise(bunch[1], 1)
+            columns_bc(first)
+            sort_loads(3)
+            u = first + 1
+            columns_a(u)
+            sort_loads(1)
+            if u < UNITS - 1:
+                columns_bc(u)
+            else:
+                store(u, 0, 512)
+                for n0 in (512, 640):
+                    bank, acc = take_bank([P, 128], "acc_last")
+                    group(acc[:], u, n0, 128)
+                    evacuate(u, acc[:], n0, n0 + 128)
+                    give_bank(bank)
+                    store(u, n0, n0 + 128)

@@ -24,6 +24,7 @@ LOAD_K = 2 * K_PASS
 UNITS = ROUNDS * TILES
 PARTS = ((0, 4), (4, 2))
 BANKS = 8
+BUNCHES = ((3, 4), (5, 6, 7), (8, 9, 10), (11, 12, 13), (14, 15))
 
 FLOPS = 2 * TOKENS * D * E
 
@@ -36,8 +37,8 @@ def tile_longcatrouter_kernel(tc, hidden_states, weight_words, weight_scales, ou
         const = ctx.enter_context(tc.tile_pool(name="const", bufs=1))
         raw_pool = ctx.enter_context(tc.tile_pool(name="raw", bufs=1))
         srt_pool = ctx.enter_context(tc.tile_pool(name="srt", bufs=12))
-        grp_pool = ctx.enter_context(tc.tile_pool(name="grp", bufs=3))
-        code_pool = ctx.enter_context(tc.tile_pool(name="code", bufs=4))
+        grp_pool = ctx.enter_context(tc.tile_pool(name="grp", bufs=4))
+        code_pool = ctx.enter_context(tc.tile_pool(name="code", bufs=6))
         psum = ctx.enter_context(tc.psum_pool(name="psum", bufs=1))
         ctx.enter_context(tc.manual_schedule())
 
@@ -238,29 +239,33 @@ def tile_longcatrouter_kernel(tc, hidden_states, weight_words, weight_scales, ou
         give_bank(bank_c1)
         sort_loads(3)
 
-        for first in range(2, UNITS, 2):
-            bunch = [u for u in (first + 1, first + 2) if u < UNITS]
+        nxt = 2
+        for j in range(len(BUNCHES)):
+            bunch = BUNCHES[j]
+            following = len(BUNCHES[j + 1]) * UNIT_LOADS if j + 1 < len(BUNCHES) else 0
             for u in bunch:
                 transpose_unit(u)
             quantise(bunch[0], 0)
             quantise(bunch[0], 1)
-            sort_loads(2)
-            columns_a(first)
-            if len(bunch) > 1:
-                quantise(bunch[1], 0)
-                quantise(bunch[1], 1)
-            columns_bc(first)
-            sort_loads(3)
-            u = first + 1
-            columns_a(u)
-            sort_loads(1)
-            if u < UNITS - 1:
-                columns_bc(u)
-            else:
-                store(u, 0, 512)
-                for n0 in (512, 640):
-                    bank, acc = take_bank([P, 128], "acc_last")
-                    group(acc[:], u, n0, 128)
-                    evacuate(u, acc[:], n0, n0 + 128)
-                    give_bank(bank)
-                    store(u, n0, n0 + 128)
+            todo = list(bunch[1:])
+            run = list(range(nxt, bunch[-1] if j + 1 < len(BUNCHES) else UNITS))
+            nxt = bunch[-1]
+            share = -(-following // len(run))
+            for u in run:
+                columns_a(u)
+                if todo:
+                    quantise(todo[0], 0)
+                    quantise(todo[0], 1)
+                    todo = todo[1:]
+                if u < UNITS - 1:
+                    columns_bc(u)
+                else:
+                    store(u, 0, 512)
+                    for n0 in (512, 640):
+                        bank, acc = take_bank([P, 128], "acc_last")
+                        group(acc[:], u, n0, 128)
+                        evacuate(u, acc[:], n0, n0 + 128)
+                        give_bank(bank)
+                        store(u, n0, n0 + 128)
+                sort_loads(min(share, following))
+                following -= min(share, following)

@@ -24,7 +24,6 @@ LOAD_K = 2 * K_PASS
 UNITS = ROUNDS * TILES
 PARTS = ((0, 4), (4, 2))
 BANKS = 8
-BUNCHES = ((3, 4), (5, 6, 7), (8, 9, 10), (11, 12, 13), (14, 15))
 
 FLOPS = 2 * TOKENS * D * E
 
@@ -37,10 +36,9 @@ def tile_longcatrouter_kernel(tc, hidden_states, weight_words, weight_scales, ou
         const = ctx.enter_context(tc.tile_pool(name="const", bufs=1))
         raw_pool = ctx.enter_context(tc.tile_pool(name="raw", bufs=1))
         srt_pool = ctx.enter_context(tc.tile_pool(name="srt", bufs=12))
-        grp_pool = ctx.enter_context(tc.tile_pool(name="grp", bufs=4))
-        code_pool = ctx.enter_context(tc.tile_pool(name="code", bufs=6))
+        grp_pool = ctx.enter_context(tc.tile_pool(name="grp", bufs=3))
+        code_pool = ctx.enter_context(tc.tile_pool(name="code", bufs=4))
         psum = ctx.enter_context(tc.psum_pool(name="psum", bufs=1))
-        ctx.enter_context(tc.manual_schedule())
 
         w_scales = []
         for r in range(ROUNDS):
@@ -239,33 +237,29 @@ def tile_longcatrouter_kernel(tc, hidden_states, weight_words, weight_scales, ou
         give_bank(bank_c1)
         sort_loads(3)
 
-        nxt = 2
-        for j in range(len(BUNCHES)):
-            bunch = BUNCHES[j]
-            following = len(BUNCHES[j + 1]) * UNIT_LOADS if j + 1 < len(BUNCHES) else 0
+        for first in range(2, UNITS, 2):
+            bunch = [u for u in (first + 1, first + 2) if u < UNITS]
             for u in bunch:
                 transpose_unit(u)
             quantise(bunch[0], 0)
             quantise(bunch[0], 1)
-            todo = list(bunch[1:])
-            run = list(range(nxt, bunch[-1] if j + 1 < len(BUNCHES) else UNITS))
-            nxt = bunch[-1]
-            share = -(-following // len(run))
-            for u in run:
-                columns_a(u)
-                if todo:
-                    quantise(todo[0], 0)
-                    quantise(todo[0], 1)
-                    todo = todo[1:]
-                if u < UNITS - 1:
-                    columns_bc(u)
-                else:
-                    store(u, 0, 512)
-                    for n0 in (512, 640):
-                        bank, acc = take_bank([P, 128], "acc_last")
-                        group(acc[:], u, n0, 128)
-                        evacuate(u, acc[:], n0, n0 + 128)
-                        give_bank(bank)
-                        store(u, n0, n0 + 128)
-                sort_loads(min(share, following))
-                following -= min(share, following)
+            sort_loads(2)
+            columns_a(first)
+            if len(bunch) > 1:
+                quantise(bunch[1], 0)
+                quantise(bunch[1], 1)
+            columns_bc(first)
+            sort_loads(3)
+            u = first + 1
+            columns_a(u)
+            sort_loads(1)
+            if u < UNITS - 1:
+                columns_bc(u)
+            else:
+                store(u, 0, 512)
+                for n0 in (512, 640):
+                    bank, acc = take_bank([P, 128], "acc_last")
+                    group(acc[:], u, n0, 128)
+                    evacuate(u, acc[:], n0, n0 + 128)
+                    give_bank(bank)
+                    store(u, n0, n0 + 128)

from contextlib import ExitStack

import concourse.mybir as mybir
from concourse.masks import make_identity

BF16 = mybir.dt.bfloat16
F32 = mybir.dt.float32
I32 = mybir.dt.int32
U8 = mybir.dt.uint8
U32 = mybir.dt.uint32
FP8X4 = mybir.dt.float8_e4m3fn_x4
FP4X4 = mybir.dt.float4_e2m1fn_x4
ADD = mybir.AluOpType.add

P = 128
TOKENS, D, E = 1024, 6144, 768
K_PASS = 512
TILES = TOKENS // P
ROUNDS = 2
UNIT_PASSES = 6
UNIT_K = UNIT_PASSES * K_PASS
UNIT_LOADS = UNIT_PASSES // 2
LOAD_K = 2 * K_PASS
UNITS = ROUNDS * TILES
PARTS = ((0, 4), (4, 2))
BANKS = 8

FLOPS = 2 * TOKENS * D * E

RAW_SPLITS = {0: (4, 2), 1: (4, 2), 2: (4, 2)}


def tile_longcatrouter_kernel(tc, hidden_states, weight_words, weight_scales, out):
    nc = tc.nc
    with ExitStack() as ctx:
        const = ctx.enter_context(tc.tile_pool(name="const", bufs=1))
        raw_pool = ctx.enter_context(tc.tile_pool(name="raw", bufs=1))
        srt_pool = ctx.enter_context(tc.tile_pool(name="srt", bufs=12))
        grp_pool = ctx.enter_context(tc.tile_pool(name="grp", bufs=3))
        code_pool = ctx.enter_context(tc.tile_pool(name="code", bufs=4))
        psum = ctx.enter_context(tc.psum_pool(name="psum", bufs=1))

        w_scales = []
        for r in range(ROUNDS):
            t = const.tile([P, UNIT_PASSES, E], U8, align_bytes=64, name="w_scales_%d" % r)
            nc.vector.memset(t[:].rearrange("p g n -> p (g n)").bitcast(I32), 0)
            w_scales.append(t)
        ident = const.tile([P, P], F32, name="ident")
        make_identity(nc, ident[:])

        x_raw = {}

        def load_x(u):
            r, i = u // TILES, u % TILES
            first = 0
            for passes in RAW_SPLITS.get(u, (UNIT_PASSES,)):
                t = raw_pool.tile([P, passes * K_PASS], BF16, name="x_raw_%d_%d" % (u, first))
                k0 = r * UNIT_K + first * K_PASS
                nc.sync.dma_start(out=t[:], in_=hidden_states[P * i : P * (i + 1), k0 : k0 + passes * K_PASS])
                for j in range(passes // 2):
                    x_raw[(u, first // 2 + j)] = t[:, LOAD_K * j : LOAD_K * (j + 1)]
                first += passes

        scales_by_row = weight_scales.rearrange("g q n -> q g n")

        def load_scales(r):
            g0 = r * UNIT_PASSES
            for row in range(4):
                nc.sync.dma_start(
                    out=w_scales[r][row:P:32, :, :].bitcast(I32),
                    in_=scales_by_row[row:16:4, g0 : g0 + UNIT_PASSES, :].bitcast(I32),
                )

        words_by_part = weight_words.rearrange("g p b -> p g b")
        w_words = {}

        def load_words(g0, g1):
            t = const.tile([P, g1 - g0, 2 * E], U8, align_bytes=64, name="w_words_%d" % g0)
            nc.sync.dma_start(out=t[:].bitcast(I32), in_=words_by_part[:, g0:g1, :].bitcast(I32))
            for g in range(g0, g1):
                w_words[g] = (t, g - g0)

        load_x(0)
        load_x(1)
        load_scales(0)
        load_words(0, 1)
        load_words(1, 3)
        load_x(2)
        load_words(3, 6)
        for u in range(3, TILES):
            load_x(u)
        load_scales(1)
        load_words(6, 9)
        load_words(9, 12)
        for u in range(TILES, UNITS):
            load_x(u)

        sums = [const.tile([P, E], F32, name="sums_%d" % i) for i in range(TILES)]

        x_srt = {}
        grouped = {}
        codes = {}
        x_scales = {}
        state = {"free": list(range(BANKS)), "sorted": 0}

        def take_bank(shape, name):
            bank = state["free"][0]
            state["free"] = state["free"][1:]
            return bank, psum.tile(shape, F32, tag="bank%d" % bank, name=name)

        def give_bank(bank):
            state["free"] = state["free"] + [bank]

        def sort_loads(count):
            for n in range(state["sorted"], min(state["sorted"] + count, UNITS * UNIT_LOADS)):
                t = srt_pool.tile([P, 2, 2, P], F32, tag="x_srt", name="x_srt")
                nc.vector.tensor_copy(
                    out=t[:],
                    in_=x_raw[(n // UNIT_LOADS, n % UNIT_LOADS)]
                    .bitcast(F32)
                    .rearrange("t (g q u) -> t g u q", g=2, q=P, u=2),
                )
                x_srt[(n // UNIT_LOADS, n % UNIT_LOADS)] = t
            state["sorted"] = state["sorted"] + count

        def transpose_load(u, l, eng):
            bank, pt = take_bank([P, 4, P], "pt")
            for j in range(4):
                nc.tensor.transpose(pt[:, j, :], x_srt[(u, l)][:, j // 2, j % 2, :], ident[:])
            part = 0 if l < 2 else 1
            if l in (0, 2):
                grouped[(u, part)] = grp_pool.tile(
                    [P, PARTS[part][1] * K_PASS], BF16, tag="grouped%d" % part, name="grouped", align_bytes=64
                )
            at = LOAD_K * (l % 2)
            dst = grouped[(u, part)][:, at : at + LOAD_K].bitcast(F32).rearrange("p (g t u) -> p g t u", g=2, t=P, u=2)
            src = pt[:].rearrange("p (g u) t -> p g t u", u=2)
            if eng == "S":
                nc.scalar.copy(out=dst, in_=src)
            else:
                nc.vector.tensor_copy(out=dst, in_=src)
            give_bank(bank)

        def transpose_unit(u, engines="SSS"):
            for l in range(UNIT_LOADS):
                transpose_load(u, l, engines[l])

        def quantise(u, part):
            width = PARTS[part][1] * P
            c = code_pool.tile([P, width], U32, tag="codes%d" % part, name="codes", align_bytes=64)
            s = code_pool.tile([P, width], U8, tag="x_scales%d" % part, name="x_scales", align_bytes=64)
            nc.vector.quantize_mx(out=c[:].bitcast(FP8X4), scales=s[:], in_=grouped[(u, part)][:])
            codes[(u, part)] = c
            x_scales[(u, part)] = s

        def mx(acc, u, gl, n0, n):
            r = u // TILES
            part = 0 if gl < 4 else 1
            at = P * (gl - PARTS[part][0])
            wt, wg = w_words[r * UNIT_PASSES + gl]
            nc.tensor.matmul_mx(
                out=acc,
                lhsT=codes[(u, part)][:, at : at + P].bitcast(FP8X4),
                lhsT_scale=x_scales[(u, part)][:, at : at + P],
                rhs=wt[:, wg, 2 * n0 : 2 * (n0 + n)].bitcast(FP4X4),
                rhs_scale=w_scales[r][:, gl, n0 : n0 + n],
                start=(gl == 0),
                stop=(gl == UNIT_PASSES - 1),
            )

        def group(acc, u, n0, n):
            for gl in range(UNIT_PASSES):
                mx(acc, u, gl, n0, n)

        def evacuate(u, acc, c0, c1, eng="V"):
            dst = sums[u % TILES][:, c0:c1]
            if u >= TILES:
                nc.vector.tensor_tensor(out=dst, in0=acc, in1=dst, op=ADD)
            elif eng == "S":
                nc.scalar.copy(out=dst, in_=acc)
            else:
                nc.vector.tensor_copy(out=dst, in_=acc)

        def store(u, c0, c1):
            i = u % TILES
            nc.sync.dma_start(out=out[P * i : P * (i + 1), c0:c1], in_=sums[i][:, c0:c1])

        def columns_a(u):
            bank, acc = take_bank([P, 512], "acc_a")
            group(acc[:], u, 0, 512)
            evacuate(u, acc[:], 0, 512)
            give_bank(bank)

        def columns_bc(u):
            bank, acc = take_bank([P, 256], "acc_bc")
            group(acc[:, 0:128], u, 512, 128)
            group(acc[:, 128:256], u, 640, 128)
            evacuate(u, acc[:], 512, 768)
            give_bank(bank)
            if u >= TILES:
                store(u, 0, E)

        sort_loads(6)
        transpose_unit(0)
        quantise(0, 0)
        quantise(0, 1)
        transpose_unit(1)
        quantise(1, 0)
        quantise(1, 1)
        sort_loads(3)

        head = []
        for u, n0, n in ((0, 0, 512), (0, 512, 128), (0, 640, 128), (1, 0, 512), (1, 512, 128)):
            bank, acc = take_bank([P, n], "acc_head")
            head.append((u, n0, n, bank, acc))
        for gl in range(3):
            for u, n0, n, bank, acc in head:
                mx(acc[:], u, gl, n0, n)
        transpose_unit(2)
        quantise(2, 0)
        quantise(2, 1)
        sort_loads(3)
        for gl in range(3, UNIT_PASSES):
            for u, n0, n, bank, acc in head:
                mx(acc[:], u, gl, n0, n)
        for at in (1, 4, 2):
            u, n0, n, bank, acc = head[at]
            evacuate(u, acc[:], n0, n0 + n, "V" if u == 0 else "S")
            give_bank(bank)
        bank_c1, acc_c1 = take_bank([P, 128], "acc_head")
        group(acc_c1[:], 1, 640, 128)
        for at in (0, 3):
            u, n0, n, bank, acc = head[at]
            evacuate(u, acc[:], n0, n0 + n, "V" if u == 0 else "S")
            give_bank(bank)
        evacuate(1, acc_c1[:], 640, 768, "S")
        give_bank(bank_c1)
        sort_loads(3)

        for first in range(2, UNITS, 2):
            bunch = [u for u in (first + 1, first + 2) if u < UNITS]
            for u in bunch:
                transpose_unit(u)
            quantise(bunch[0], 0)
            quantise(bunch[0], 1)
            sort_loads(2)
            columns_a(first)
            if len(bunch) > 1:
                quantise(bunch[1], 0)
                quantise(bunch[1], 1)
            columns_bc(first)
            sort_loads(3)
            u = first + 1
            columns_a(u)
            sort_loads(1)
            if u < UNITS - 1:
                columns_bc(u)
            else:
                store(u, 0, 512)
                for n0 in (512, 640):
                    bank, acc = take_bank([P, 128], "acc_last")
                    group(acc[:], u, n0, 128)
                    evacuate(u, acc[:], n0, n0 + 128)
                    give_bank(bank)
                    store(u, n0, n0 + 128)
